import numpy as np
import ml_dtypes


def mxq(x, axis, fmt="e4m3"):
    dtype, down = {"e4m3": (ml_dtypes.float8_e4m3fn, 7), "e5m2": (ml_dtypes.float8_e5m2, 14)}[fmt]
    v = np.moveaxis(np.asarray(x, np.float32).astype(ml_dtypes.bfloat16).astype(np.float64), axis, -1)
    blocks = v.reshape(v.shape[:-1] + (-1, 32))
    amax = np.abs(blocks).max(-1, keepdims=True)
    byte = np.maximum(np.where(amax > 0, np.frexp(amax)[1] - 1 + 127, 0) - down, 1)
    scale = np.exp2(byte - 127.0)
    codes = (blocks / scale).astype(np.float32).astype(dtype).astype(np.float64)
    return np.moveaxis((codes * scale).reshape(v.shape), -1, axis)


WIDE = False


def mx_kscale(k):
    if not WIDE:
        return np.ones(k)
    levels = np.array([18, -18])
    if k % 512:
        return np.exp2(np.random.permutation(np.resize(levels, k // 32))).repeat(32)
    a = np.empty((k // 512, 16))
    for p in range(k // 512):
        a[p, :8] = np.random.permutation(np.resize(levels, 8))
        for g in range(8):
            far = levels[np.abs(levels - a[p, g]) >= 10]
            a[p, g + 8] = far[np.random.randint(len(far))]
    return np.exp2(a.ravel()).repeat(32)


BF16 = ml_dtypes.bfloat16


def bf(x):
    return np.asarray(x, np.float32).astype(BF16)


def f64(x):
    return np.asarray(x).astype(np.float64)


B, E, D = 1024, 512, 1024


def mix(x, state_x, m):
    return x * m + state_x * (1.0 - m)


def grad_draw(s, u):
    e = np.exp2(np.random.randint(-6, 1, (B, 1)))
    return bf(np.random.standard_normal((B, D)) * e / s * u)


def setup_inputs():
    s = mx_kscale(B)[:, None]
    u = mx_kscale(D)
    ws = 1.0 / np.sqrt(E)
    x0 = bf(np.random.standard_normal((B, E)))
    state_A = bf(np.random.uniform(0.0, 1.0, (B, D)))
    state_B = bf(0.5 + np.random.uniform(0.0, 1.0, (B, D)))
    state_p = bf(np.random.standard_normal((B, D)))
    state_x0 = bf(np.random.standard_normal((B, E)))
    time_decay = bf(0.5 * np.random.standard_normal(D))
    time_first = bf(np.log(0.3) + 0.3 * np.random.standard_normal(D))
    time_mix_k = bf(np.random.uniform(0.0, 1.0, (1, E)))
    time_mix_v = bf(np.random.uniform(0.0, 1.0, (1, E)))
    W_key0 = bf(np.random.standard_normal((D, E)) * ws)
    W_value0 = bf(np.random.standard_normal((D, E)) * ws)
    k = mix(f64(x0), f64(state_x0), f64(time_mix_k)) @ f64(W_key0).T
    v = mix(f64(x0), f64(state_x0), f64(time_mix_v)) @ f64(W_value0).T
    for _ in range(6):
        sp = f64(state_p)
        near = (np.abs(sp - f64(time_first) - k) < 1.0 / 64) | (np.abs(sp - np.exp(f64(time_decay)) - k) < 1.0 / 64)
        state_p = bf(np.where(near, sp + 0.125, sp))
    return {
        "x": bf(f64(x0) * s),
        "state_A": state_A,
        "state_B": state_B,
        "state_p": state_p,
        "state_x": bf(f64(state_x0) * s),
        "time_decay": time_decay,
        "time_first": time_first,
        "time_mix_k": time_mix_k,
        "time_mix_v": time_mix_v,
        "W_key": bf(f64(W_key0) / u[:, None]),
        "W_value": bf(f64(W_value0) / u[:, None]),
        "k": np.asarray(k, np.float32),
        "v": np.asarray(v, np.float32),
        "grad_0": grad_draw(s, u),
        "grad_1": grad_draw(s, u),
        "grad_2": grad_draw(s, u),
        "grad_3": grad_draw(s, u),
        "grad_4": grad_draw(s, u),
    }


def reference(x, state_A, state_B, state_p, state_x, time_decay, time_first, time_mix_k, time_mix_v, W_key, W_value,
              k, v, grad_0, grad_1, grad_2, grad_3, grad_4):
    x, state_x = f64(x), f64(state_x)
    sA, sB, sp = f64(state_A), f64(state_B), f64(state_p)
    mk, mv = f64(time_mix_k), f64(time_mix_v)
    kf, vf = f64(k), f64(v)
    g0, g1, g2, g3, g4 = f64(grad_0), f64(grad_1), f64(grad_2), f64(grad_3), f64(grad_4)
    ww = f64(time_first) + kf
    p = np.maximum(sp, ww)
    e1 = np.exp(sp - p)
    e2 = np.exp(ww - p)
    dk_out = np.where(ww > sp, -(g0 * sA + g1 * sB) * e1, (g0 * vf + g1) * e2)
    ww2 = sp - np.exp(f64(time_decay))
    p2 = np.maximum(ww2, kf)
    f1 = np.exp(ww2 - p2)
    f2 = np.exp(kf - p2)
    dk_state = np.where(kf > ww2, g4 - (g2 * sA + g3 * sB) * f1, (g2 * vf + g3) * f2)
    dk = dk_out + dk_state
    dv = g0 * e2 + g2 * f2
    dkv = np.concatenate([dk, dv], axis=1)
    wm = np.concatenate([f64(W_key) * mk, f64(W_value) * mv], axis=0)
    dx = mxq(dkv, 1, "e5m2") @ mxq(wm, 0, "e4m3")
    xk = mix(x, state_x, mk)
    xv = mix(x, state_x, mv)
    dwk = mxq(dk, 0, "e5m2").T @ mxq(xk, 0, "e4m3")
    dwv = mxq(dv, 0, "e5m2").T @ mxq(xv, 0, "e4m3")
    return dx, dwk, dwv

@@ -1,0 +1,487 @@
+from contextlib import ExitStack
+
+import concourse.mybir as mybir
+from concourse.masks import make_identity
+
+B, E, D = 1024, 512, 1024
+FLOPS = 2 * B * 2 * D * E + 2 * 2 * B * D * E
+
+F32 = mybir.dt.float32
+BF16 = mybir.dt.bfloat16
+U32 = mybir.dt.uint32
+U8 = mybir.dt.uint8
+E4M3 = mybir.dt.float8_e4m3fn_x4
+E5M2 = mybir.dt.float8_e5m2_x4
+ALU = mybir.AluOpType
+ACT = mybir.ActivationFunctionType
+
+P = 128
+PACK = 4
+KP = P * PACK
+UNITS = 16
+LOAD_W = 256
+
+
+def tile_rwkv_timemix_for_quant_pa_v_kernel(
+    tc, x, state_A, state_B, state_p, state_x, time_decay, time_first, time_mix_k, time_mix_v,
+    W_key, W_value, k, v, grad_0, grad_1, grad_2, grad_3, grad_4, out_0, out_1, out_2,
+):
+    nc = tc.nc
+    src = {"k": k, "sp": state_p, "sA": state_A, "v": v, "sB": state_B,
+           "g1": grad_1, "g3": grad_3, "g0": grad_0, "g2": grad_2, "g4": grad_4}
+    weights = (W_key, W_value)
+    outs_w = (out_1, out_2)
+
+    with ExitStack() as ctx:
+        keep = ctx.enter_context(tc.tile_pool(name="keep", bufs=1))
+        sb = ctx.enter_context(tc.tile_pool(name="sb", bufs=2))
+        ps = ctx.enter_context(tc.psum_pool(name="ps", bufs=1))
+        ctx.enter_context(tc.manual_schedule())
+
+        loaded = {}
+        T = {}
+        count = {"fwd": 0, "back": 0}
+
+        def bank(kind, dtype):
+            if kind == "fwd":
+                tag = "fwd%d" % (count["fwd"] % 4)
+                count["fwd"] = count["fwd"] + 1
+            elif kind == "back":
+                tag = "back%d" % (count["back"] % 3)
+                count["back"] = count["back"] + 1
+            else:
+                tag = kind
+            width = KP if dtype == F32 else 2 * KP
+            return ps.tile([P, width], dtype, tag=tag, name=tag)
+
+        def load(name, sc):
+            if sc >= UNITS // 2:
+                return
+            g, q = divmod(sc, 4)
+            t = sb.tile([P, PACK, LOAD_W], src[name].dtype, tag="in_" + name, name="in_" + name)
+            rows = src[name][g * KP:(g + 1) * KP, q * LOAD_W:(q + 1) * LOAD_W]
+            nc.sync.dma_start(out=t[:], in_=rows.rearrange("(p j) w -> p j w", j=PACK))
+            loaded[name, sc] = t
+
+        def cols(name, u):
+            h = u % 2
+            return loaded[name, u // 2][:, :, h * P:(h + 1) * P]
+
+        def release(u, *names):
+            if u % 2 == 1:
+                for name in names:
+                    load(name, u // 2 + 2)
+
+        def transpose_sum(dst, terms):
+            for j in range(PACK):
+                for i, term in enumerate(terms):
+                    nc.tensor.matmul(dst[:, j * P:(j + 1) * P], lhsT=term(j), rhs=ident32[:], is_transpose=True,
+                                     start=(i == 0), stop=(i == len(terms) - 1))
+
+        def transpose_bf16(dst, name, u):
+            for j in range(PACK):
+                nc.tensor.transpose(dst[:, j * P:(j + 1) * P], cols(name, u)[:, j, :], ident16[:])
+
+        def twice(ap):
+            return ap.unsqueeze(1).broadcast_to([P, 2, KP])
+
+        rows = keep.tile([P, P], BF16)
+        nc.vector.memset(rows[:], 0.0)
+        nc.sync.dma_start(out=rows[0:8, :], in_=time_first.rearrange("(c p) -> c p", p=P))
+        nc.sync.dma_start(out=rows[8:16, :], in_=time_decay.rearrange("(c p) -> c p", p=P))
+        nc.sync.dma_start(out=rows[16:20, :], in_=time_mix_k.rearrange("o (c p) -> (o c) p", p=P))
+        nc.sync.dma_start(out=rows[20:24, :], in_=time_mix_v.rearrange("o (c p) -> (o c) p", p=P))
+        ident16 = keep.tile([P, P], BF16)
+        ident32 = keep.tile([P, P], F32)
+        make_identity(nc, ident16[:])
+        make_identity(nc, ident32[:])
+
+        wm_codes = keep.tile([P, 4, E], U32, align_bytes=64)
+        wm_scales = keep.tile([P, 4, E], U8, align_bytes=64)
+        xm_codes = keep.tile([P, 4, E], U32, align_bytes=64)
+        xm_scales = keep.tile([P, 4, E], U8, align_bytes=64)
+        colv = keep.tile([P, 24], F32)
+        decay = keep.tile([P, 8], F32)
+        mix = keep.tile([P, 2, E], F32)
+
+        def load_w(i):
+            t, fg = divmod(i, 2)
+            w = sb.tile([P, PACK, E], BF16, tag="w_raw", name="w_raw", bufs=1)
+            nc.sync.dma_start(out=w[:], in_=weights[t][fg * KP:(fg + 1) * KP, :].rearrange("(q j) e -> q j e", j=PACK))
+            T["w", i] = w
+
+        def load_x(i):
+            g, eh = divmod(i, 2)
+            for name, a in (("x", x), ("sx", state_x)):
+                t = sb.tile([P, PACK, E // 2], BF16, tag=name, name=name)
+                part = a[g * KP:(g + 1) * KP, eh * (E // 2):(eh + 1) * (E // 2)]
+                nc.sync.dma_start(out=t[:], in_=part.rearrange("(p j) w -> p j w", j=PACK))
+                T[name, i] = t
+
+        load("k", 0)
+        load("sp", 0)
+        load_w(0)
+        for name in ("sA", "v", "sB", "g1", "g3", "g0", "g2", "g4"):
+            load(name, 0)
+        load_x(0)
+        for name in ("sp", "sA", "sB", "k", "v", "g1", "g3", "g0", "g2", "g4"):
+            load(name, 1)
+        load_x(1)
+
+        small = bank("back", BF16)
+        nc.tensor.transpose(small[:, 0:P], rows[:], ident16[:])
+        nc.scalar.activation(decay[:], small[:, 8:16], ACT.Exp)
+        nc.scalar.copy(colv[:], small[:, 0:24])
+        for t in range(2):
+            spread = bank("back", F32)
+            for c in range(4):
+                col = colv[:, 16 + 4 * t + c:17 + 4 * t + c]
+                nc.tensor.transpose(spread[:, c * P:(c + 1) * P], col.to_broadcast([P, P]), ident32[:])
+            nc.vector.tensor_copy(mix[:, t, :], spread[:])
+
+        def grouped():
+            return sb.tile([P, E, PACK], BF16, tag="grouped", name="grouped", bufs=3, align_bytes=64)
+
+        def wm_mult(i):
+            t = i // 2
+            gr = grouped()
+            nc.vector.tensor_tensor(gr[:], T["w", i][:].rearrange("q j e -> q e j"),
+                                    mix[:, t, :].unsqueeze(2).broadcast_to([P, E, PACK]), ALU.mult)
+            T["wg", i] = gr
+            if i + 1 < 4:
+                load_w(i + 1)
+
+        def wm_quant(i):
+            nc.vector.quantize_mx(out=wm_codes[:, i, :].bitcast(E4M3), scales=wm_scales[:, i, :],
+                                  in_=T["wg", i][:].rearrange("q e j -> q (e j)"))
+
+        def x_piece(n):
+            i, step = divmod(n, 3)
+            eh = i % 2
+            if step == 0:
+                dx = sb.tile([P, PACK, E // 2], F32, tag="dx", name="dx", bufs=1)
+                nc.gpsimd.tensor_tensor(dx[:], T["x", i][:], T["sx", i][:], ALU.subtract)
+                T["dx", i] = dx
+            else:
+                t = step - 1
+                md = sb.tile([P, PACK, E // 2], F32, tag="md", name="md")
+                m = mix[:, t, eh * (E // 2):(eh + 1) * (E // 2)]
+                nc.gpsimd.tensor_tensor(md[:], T["dx", i][:], m.unsqueeze(1).broadcast_to([P, PACK, E // 2]), ALU.mult)
+                T["md", i, t] = md
+
+        def x_add(i, t):
+            g, eh = divmod(i, 2)
+            if eh == 0:
+                T["xg", g, t] = grouped()
+            dst = T["xg", g, t][:, eh * (E // 2):(eh + 1) * (E // 2), :]
+            nc.vector.tensor_tensor(dst, T["md", i, t][:].rearrange("p j e -> p e j"),
+                                    T["sx", i][:].rearrange("p j e -> p e j"), ALU.add)
+            if t == 1 and i + 2 < 4:
+                load_x(i + 2)
+
+        def x_quant(g, t):
+            nc.vector.quantize_mx(out=xm_codes[:, 2 * g + t, :].bitcast(E4M3), scales=xm_scales[:, 2 * g + t, :],
+                                  in_=T["xg", g, t][:].rearrange("p e j -> p (e j)"))
+
+        def casts(u):
+            if u >= UNITS:
+                return
+            for name, scale, bias in (("sp", -1.0, 0.0), ("sA", 1.0, 0.0), ("sB", -1.0, -1.0)):
+                c = sb.tile([P, PACK, P], F32, tag="c_" + name, name="c_" + name)
+                nc.scalar.activation(c[:], cols(name, u), ACT.Copy, bias=bias, scale=scale)
+                T["c_" + name, u] = c
+            release(u, "sp", "sA", "sB")
+
+        def fill_s(u):
+            if u >= UNITS:
+                return
+            s = bank("s", F32)
+            transpose_sum(s, [lambda j: cols("k", u)[:, j, :], lambda j: T["c_sp", u][:, j, :]])
+            T["s", u] = s
+            release(u, "k")
+
+        def exps_read(u):
+            if u >= UNITS:
+                return
+            fb = u % 8
+            bias = (colv[:, fb:fb + 1], decay[:, fb:fb + 1])
+            xe = sb.tile([P, 2, KP], F32, tag="xe", name="xe")
+            ee = sb.tile([P, 2, KP], F32, tag="ee", name="ee", bufs=3)
+            for h in range(2):
+                nc.scalar.activation(xe[:, h, :], T["s", u][:], ACT.Exp, bias=bias[h])
+            for h in range(2):
+                nc.scalar.activation(ee[:, h, :], T["s", u][:], ACT.Abs, bias=bias[h])
+            T["xe", u] = xe
+            T["ee", u] = ee
+
+        def exps_rest(u):
+            if u >= UNITS:
+                return
+            ee = T["ee", u]
+            nc.scalar.activation(ee[:], ee[:], ACT.Exp, scale=-1.0)
+
+        def fill(what, u):
+            if u >= UNITS:
+                return
+            if what == "vA":
+                b = bank("fwd", F32)
+                transpose_sum(b, [lambda j: cols("v", u)[:, j, :], lambda j: T["c_sA", u][:, j, :]])
+            elif what == "nsB":
+                b = bank("fwd", F32)
+                transpose_sum(b, [lambda j: T["c_sB", u][:, j, :]])
+            elif what == "v":
+                b = bank("fwd", F32)
+                transpose_sum(b, [lambda j: cols("v", u)[:, j, :]])
+                release(u, "v")
+            else:
+                names = {"g13": ("g1", "g3"), "g02": ("g0", "g2"), "g4": ("g4",)}[what]
+                b = bank("fwd", BF16)
+                for h, name in enumerate(names):
+                    transpose_bf16(b[:, h * KP:(h + 1) * KP], name, u)
+                release(u, *names)
+            T[what, u] = b
+
+        def pair(ap):
+            return ap.rearrange("p (h n) -> p h n", h=2)
+
+        def op_a(u):
+            a = sb.tile([P, 2, KP], F32, tag="a", name="a")
+            nc.vector.scalar_tensor_tensor(a[:], T["xe", u][:], 1.0, twice(T["vA", u][:]), ALU.is_gt, ALU.mult)
+            T["a", u] = a
+
+        def op_d(u):
+            b = sb.tile([P, 2, KP], F32, tag="b", name="b")
+            nc.vector.scalar_tensor_tensor(b[:], T["xe", u][:], 1.0, twice(T["nsB", u][:]), ALU.is_gt, ALU.mult)
+            T["b", u] = b
+
+        def op_b(u):
+            a = T["a", u]
+            nc.vector.tensor_tensor(a[:], twice(T["v", u][:]), a[:], ALU.subtract)
+
+        def op_e(u):
+            b = T["b", u]
+            nc.vector.scalar_tensor_tensor(b[:], b[:], 1.0, pair(T["g13", u][:]), ALU.add, ALU.mult)
+
+        def op_c(u):
+            a = T["a", u]
+            nc.vector.tensor_tensor(a[:], pair(T["g02", u][:]), a[:], ALU.mult)
+
+        def op_f(u, eng):
+            a = T["a", u]
+            eng.tensor_tensor(a[:], a[:], T["b", u][:], ALU.add)
+
+        def op_g(u, eng):
+            a = T["a", u]
+            eng.tensor_tensor(a[:], a[:], T["ee", u][:], ALU.mult)
+
+        def op_h(u):
+            dvt = sb.tile([P, 2, KP], F32, tag="dvt", name="dvt")
+            nc.vector.scalar_tensor_tensor(dvt[:], T["xe", u][:], 1.0, pair(T["g02", u][:]), ALU.min, ALU.mult)
+            T["dvt", u] = dvt
+
+        def op_m(u):
+            mg = sb.tile([P, KP], F32, tag="mg", name="mg")
+            nc.vector.scalar_tensor_tensor(mg[:], T["xe", u][:, 1, :], 1.0, T["g4", u][:, 0:KP], ALU.is_gt, ALU.mult)
+            T["mg", u] = mg
+
+        def back(t, u, kind="back"):
+            if u < 0:
+                return
+            b = bank(kind, F32)
+            if t == 0:
+                a, mg = T["a", u], T["mg", u]
+                terms = [lambda j: mg[:, j * P:(j + 1) * P], lambda j: a[:, 0, j * P:(j + 1) * P],
+                         lambda j: a[:, 1, j * P:(j + 1) * P]]
+            else:
+                dvt = T["dvt", u]
+                terms = [lambda j: dvt[:, 0, j * P:(j + 1) * P], lambda j: dvt[:, 1, j * P:(j + 1) * P]]
+            transpose_sum(b, terms)
+            T["back", t, u] = b
+
+        def x_copy(t, u):
+            if u < 0:
+                return
+            c, fbl = divmod(u, 4)
+            if ("xx", c) not in T:
+                T["xx", c] = sb.tile([P, 2, KP * PACK], BF16, tag="xx", name="xx", align_bytes=64)
+            dst = T["xx", c][:, t, :].rearrange("p (jp f q j) -> p jp f q j", jp=PACK, f=4, j=PACK)[:, :, fbl, :, :]
+            nc.scalar.copy(dst, T["back", t, u][:].rearrange("p (j q jp) -> p jp q j", j=PACK, jp=PACK))
+
+        def quant(name, c, ts):
+            if (name + "c", c) not in T:
+                nb = 3 if name == "xx" else 2
+                T[name + "c", c] = sb.tile([P, 2 * KP], U32, tag=name + "c", name=name + "c", bufs=nb, align_bytes=64)
+                T[name + "s", c] = sb.tile([P, 2 * KP], U8, tag=name + "s", name=name + "s", bufs=nb, align_bytes=64)
+            lo, hi = ts[0], ts[-1] + 1
+            nc.vector.quantize_mx(out=T[name + "c", c][:, lo * KP:hi * KP].bitcast(E5M2),
+                                  scales=T[name + "s", c][:, lo * KP:hi * KP],
+                                  in_=T[name, c][:].rearrange("p t n -> p (t n)")[:, lo * KP * PACK:hi * KP * PACK])
+
+        def y_fill(c, t, w, kind="back"):
+            b = bank(kind, F32)
+            words = T["xx", c][:, t, :].bitcast(F32)
+            for jp in range(PACK):
+                nc.tensor.transpose(b[:, jp * P:(jp + 1) * P], words[:, 2 * P * jp + w:2 * P * (jp + 1):2], ident32[:])
+            T["yb", c, t, w] = b
+
+        def y_copy(c, t, w, eng="s"):
+            if ("yy", c) not in T:
+                T["yy", c] = sb.tile([P, 2, KP * PACK], BF16, tag="yy", name="yy", bufs=1, align_bytes=64)
+            dst = T["yy", c][:, t, w * 2 * KP:(w + 1) * 2 * KP].rearrange("q (e p jp) -> q e p jp", e=2, jp=PACK)
+            s = T["yb", c, t, w][:].bitcast(BF16).rearrange("q (jp p e) -> q e p jp", jp=PACK, e=2)
+            if eng == "s":
+                nc.scalar.copy(dst, s)
+            else:
+                nc.vector.tensor_copy(dst, s)
+
+        def mx(acc, name, c, t, m, codes, scales, i, start, stop):
+            lo = t * KP + m * P
+            nc.tensor.matmul_mx(out=acc[:], lhsT=T[name + "c", c][:, lo:lo + P].bitcast(E5M2),
+                                lhsT_scale=T[name + "s", c][:, lo:lo + P],
+                                rhs=codes[:, i, :].bitcast(E4M3), rhs_scale=scales[:, i, :], start=start, stop=stop)
+
+        def dx_passes(g, m, fgs, kind="back"):
+            if ("o0", g, m) not in T:
+                T["o0", g, m] = bank(kind, F32)
+            for fg in fgs:
+                for t in range(2):
+                    mx(T["o0", g, m], "yy", 2 * g + fg, t, m, wm_codes, wm_scales, 2 * t + fg,
+                       fg == 0 and t == 0, fg == 1 and t == 1)
+
+        def dw_passes(t, fg, m, kind="back"):
+            acc = bank(kind, F32)
+            for g in range(2):
+                mx(acc, "xx", 2 * g + fg, t, m, xm_codes, xm_scales, 2 * g + t, g == 0, g == 1)
+            T["ow", t, fg, m] = acc
+
+        def store(acc, dst, blk, m, eng="s"):
+            st = sb.tile([P, E], F32, tag="st", name="st", bufs=3)
+            if eng == "s":
+                nc.scalar.copy(st[:], acc[:])
+            else:
+                nc.vector.tensor_copy(st[:], acc[:])
+            nc.sync.dma_start(out=dst[blk * KP:(blk + 1) * KP, :].rearrange("(p j) e -> p j e", j=PACK)[:, m, :],
+                              in_=st[:])
+
+        def job_pe(job):
+            if job[0] == "y":
+                y_fill(*job[1:])
+            elif job[0] == "dx":
+                dx_passes(job[1], job[2], (0, 1))
+            else:
+                dw_passes(*job[1:])
+
+        def job_copy(job):
+            if job[0] == "y":
+                y_copy(*job[1:])
+            elif job[0] == "dx":
+                store(T["o0", job[1], job[2]], out_0, job[1], job[2])
+            else:
+                store(T["ow", job[1], job[2], job[3]], outs_w[job[1]], job[2], job[3])
+
+        early = {5: [("y", 0, 0, 0)], 6: [("y", 0, 0, 1)], 7: [("y", 0, 1, 0)], 8: [("y", 0, 1, 1)],
+                 9: [("y", 1, 0, 0)], 10: [("y", 1, 1, 0)], 12: [("dx", 0, 1)],
+                 13: [("y", 2, 0, 0), ("y", 2, 0, 1)], 14: [("y", 2, 1, 0), ("y", 2, 1, 1)],
+                 15: [("dw", 1, 0, 0), ("dw", 1, 0, 1)]}
+        late = {9: [("y", 1, 0, 1)], 10: [("y", 1, 1, 1)], 11: [("dx", 0, 0)], 12: [("dx", 0, 2), ("dx", 0, 3)],
+                13: [("dw", 0, 0, 0), ("dw", 0, 0, 1)], 14: [("dw", 0, 0, 2), ("dw", 0, 0, 3)],
+                15: [("dw", 1, 0, 2), ("dw", 1, 0, 3)]}
+        vec_extra = {
+            0: [lambda: wm_quant(0)],
+            1: [lambda: x_add(0, 0)], 2: [lambda: x_add(0, 1)], 3: [lambda: wm_mult(1)],
+            4: [lambda: x_add(1, 0), lambda: wm_quant(1)],
+            5: [lambda: quant("xx", 0, (0, 1)), lambda: x_add(1, 1), lambda: x_quant(0, 0)],
+            6: [lambda: x_quant(0, 1), lambda: wm_mult(2)],
+            7: [lambda: x_add(2, 0), lambda: wm_quant(2)],
+            8: [lambda: x_add(2, 1), lambda: quant("yy", 0, (0, 1))],
+            9: [lambda: quant("xx", 1, (0, 1))],
+            10: [lambda: wm_mult(3), lambda: x_add(3, 0)],
+            11: [lambda: wm_quant(3), lambda: quant("yy", 1, (0, 1)), lambda: x_add(3, 1), lambda: x_quant(1, 0)],
+            12: [lambda: x_quant(1, 1)],
+            13: [lambda: quant("xx", 2, (0, 1))],
+            15: [lambda: quant("yy", 2, (0, 1))],
+        }
+        pool_extra = {u: [u + 1] for u in range(1, 11)}
+        pool_extra[0] = [0, 1]
+
+        casts(0)
+        fill_s(0)
+        exps_read(0)
+        wm_mult(0)
+        fill("vA", 0)
+        fill("nsB", 0)
+        fill("v", 0)
+        casts(1)
+        exps_rest(0)
+        fill("g13", 0)
+
+        last = UNITS - 1
+        for u in range(UNITS):
+            fill_s(u + 1)
+            for job in early.get(u, []):
+                job_pe(job)
+            op_a(u)
+            exps_read(u + 1)
+            fill("g02", u)
+            op_d(u)
+            fill("g4", u)
+            for job in early.get(u, []):
+                job_copy(job)
+            exps_rest(u + 1)
+            back(1, u - 1)
+            x_copy(1, u - 1)
+            back(0, u - 1)
+            x_copy(0, u - 1)
+            op_b(u)
+            fill("vA", u + 1)
+            op_e(u)
+            fill("nsB", u + 1)
+            for n in pool_extra.get(u, []):
+                x_piece(n)
+            for job in vec_extra.get(u, []):
+                job()
+            for job in late.get(u, []):
+                job_pe(job)
+            op_c(u)
+            if u < last:
+                op_f(u, nc.gpsimd)
+                op_g(u, nc.gpsimd)
+            casts(u + 2)
+            for job in late.get(u, []):
+                job_copy(job)
+            op_h(u)
+            fill("v", u + 1)
+            if u == last:
+                op_f(u, nc.vector)
+            op_m(u)
+            fill("g13", u + 1)
+
+        back(1, last)
+        x_copy(1, last)
+        op_g(last, nc.vector)
+        for m in range(4):
+            dx_passes(1, m, (0,), kind="fwd")
+        y_fill(3, 1, 0)
+        y_fill(3, 1, 1, kind="s")
+        quant("xx", 3, (1,))
+        back(0, last)
+        y_copy(3, 1, 0)
+        x_copy(0, last)
+        y_copy(3, 1, 1, eng="v")
+        dw_passes(1, 1, 0)
+        dw_passes(1, 1, 1)
+        y_fill(3, 0, 0)
+        y_fill(3, 0, 1, kind="s")
+        quant("xx", 3, (0,))
+        y_copy(3, 0, 0)
+        y_copy(3, 0, 1, eng="v")
+        store(T["ow", 1, 1, 0], out_2, 1, 0)
+        store(T["ow", 1, 1, 1], out_2, 1, 1)
+        quant("yy", 3, (0, 1))
+        tiles = [(1, 2), (1, 3), (0, 0), (0, 1), (0, 2), (0, 3)]
+        for n, (t, m) in enumerate(tiles):
+            dw_passes(t, 1, m, kind=("s" if n % 4 == 3 else "back"))
+            store(T["ow", t, 1, m], outs_w[t], 1, m, eng=("s" if n % 2 == 0 else "v"))
+        for m in range(4):
+            dx_passes(1, m, (1,))
+            store(T["o0", 1, m], out_0, 1, m, eng=("s" if m % 2 == 0 else "v"))

@@ -20,6 +20,9 @@ PACK = 4
 KP = P * PACK
 UNITS = 16
 LOAD_W = 256
+WARM = 2
+PTS = ("s", "dk", "v")
+DX_ORDER = ((0, 0), (0, 1), (1, 1), (1, 0))
 
 
 def tile_rwkv_timemix_for_quant_pa_v_kernel(
@@ -54,14 +57,14 @@ def tile_rwkv_timemix_for_quant_pa_v_kernel(
             width = KP if dtype == F32 else 2 * KP
             return ps.tile([P, width], dtype, tag=tag, name=tag)
 
-        def load(name, sc):
+        def load(name, sc, lo=0, hi=LOAD_W):
             if sc >= UNITS // 2:
                 return
             g, q = divmod(sc, 4)
-            t = sb.tile([P, PACK, LOAD_W], src[name].dtype, tag="in_" + name, name="in_" + name)
-            rows = src[name][g * KP:(g + 1) * KP, q * LOAD_W:(q + 1) * LOAD_W]
-            nc.sync.dma_start(out=t[:], in_=rows.rearrange("(p j) w -> p j w", j=PACK))
-            loaded[name, sc] = t
+            if lo == 0:
+                loaded[name, sc] = sb.tile([P, PACK, LOAD_W], src[name].dtype, tag="in_" + name, name="in_" + name)
+            rows = src[name][g * KP:(g + 1) * KP, q * LOAD_W + lo:q * LOAD_W + hi]
+            nc.sync.dma_start(out=loaded[name, sc][:, :, lo:hi], in_=rows.rearrange("(p j) w -> p j w", j=PACK))
 
         def cols(name, u):
             h = u % 2
@@ -72,7 +75,11 @@ def tile_rwkv_timemix_for_quant_pa_v_kernel(
                 for name in names:
                     load(name, u // 2 + 2)
 
-        def transpose_sum(dst, terms):
+        def transpose_sum(dst, terms, warm=False):
+            for rep in range(WARM if warm else 0):
+                nc.tensor.matmul_mx(out=dst[:], lhsT=warm_codes[:].bitcast(E5M2), lhsT_scale=warm_scales[:],
+                                    rhs=wm_codes[:, 0, :].bitcast(E4M3), rhs_scale=wm_scales[:, 0, :],
+                                    start=True, stop=True)
             for j in range(PACK):
                 for i, term in enumerate(terms):
                     nc.tensor.matmul(dst[:, j * P:(j + 1) * P], lhsT=term(j), rhs=ident32[:], is_transpose=True,
@@ -100,9 +107,11 @@ def tile_rwkv_timemix_for_quant_pa_v_kernel(
         wm_scales = keep.tile([P, 4, E], U8, align_bytes=64)
         xm_codes = keep.tile([P, 4, E], U32, align_bytes=64)
         xm_scales = keep.tile([P, 4, E], U8, align_bytes=64)
+        warm_codes = keep.tile([P, P], U32, align_bytes=64)
+        warm_scales = keep.tile([P, P], U8, align_bytes=64)
         colv = keep.tile([P, 24], F32)
         decay = keep.tile([P, 8], F32)
-        mix = keep.tile([P, 2, E], F32)
+        mix = keep.tile([P, 2, E], BF16)
 
         def load_w(i):
             t, fg = divmod(i, 2)
@@ -118,15 +127,22 @@ def tile_rwkv_timemix_for_quant_pa_v_kernel(
                 nc.sync.dma_start(out=t[:], in_=part.rearrange("(p j) w -> p j w", j=PACK))
                 T[name, i] = t
 
-        load("k", 0)
-        load("sp", 0)
+        load("k", 0, 0, P)
+        load("sp", 0, 0, P)
         load_w(0)
+        for name in ("sA", "v", "sB", "g1", "g3"):
+            load(name, 0, 0, P)
+        for name in ("sp", "k"):
+            load(name, 0, P, LOAD_W)
+        for name in ("g0", "g2", "g4"):
+            load(name, 0, 0, P)
         for name in ("sA", "v", "sB", "g1", "g3", "g0", "g2", "g4"):
-            load(name, 0)
-        load_x(0)
-        for name in ("sp", "sA", "sB", "k", "v", "g1", "g3", "g0", "g2", "g4"):
+            load(name, 0, P, LOAD_W)
+        for name in ("sp", "k", "sA", "v", "sB"):
             load(name, 1)
-        load_x(1)
+        load_x(0)
+        for name in ("g1", "g3", "g0", "g2", "g4"):
+            load(name, 1)
 
         small = bank("back", BF16)
         nc.tensor.transpose(small[:, 0:P], rows[:], ident16[:])
@@ -139,17 +155,26 @@ def tile_rwkv_timemix_for_quant_pa_v_kernel(
                 nc.tensor.transpose(spread[:, c * P:(c + 1) * P], col.to_broadcast([P, P]), ident32[:])
             nc.vector.tensor_copy(mix[:, t, :], spread[:])
 
-        def grouped():
-            return sb.tile([P, E, PACK], BF16, tag="grouped", name="grouped", bufs=3, align_bytes=64)
+        def grouped(tag, bufs):
+            return sb.tile([P, E, PACK], BF16, tag=tag, name=tag, bufs=bufs, align_bytes=64)
+
+        def wm_first():
+            T["wg", 0] = grouped("wg", 1)
+            nc.vector.tensor_tensor(T["wg", 0][:], T["w", 0][:].rearrange("q j e -> q e j"),
+                                    mix[:, 0, :].unsqueeze(2).broadcast_to([P, E, PACK]), ALU.mult)
 
         def wm_mult(i):
-            t = i // 2
-            gr = grouped()
-            nc.vector.tensor_tensor(gr[:], T["w", i][:].rearrange("q j e -> q e j"),
-                                    mix[:, t, :].unsqueeze(2).broadcast_to([P, E, PACK]), ALU.mult)
-            T["wg", i] = gr
+            wp = sb.tile([P, PACK, E], BF16, tag="wp", name="wp", bufs=1)
+            nc.vector.tensor_tensor(wp[:], T["w", i][:], mix[:, i // 2, :].unsqueeze(1).broadcast_to([P, PACK, E]),
+                                    ALU.mult)
+            T["wp", i] = wp
             if i + 1 < 4:
                 load_w(i + 1)
+
+        def wm_interleave(i):
+            T["wg", i] = grouped("wg", 1)
+            nc.scalar.copy(T["wg", i][:].rearrange("q (c i) j -> q c j i", i=4),
+                           T["wp", i][:].rearrange("q j (c i) -> q c j i", i=4))
 
         def wm_quant(i):
             nc.vector.quantize_mx(out=wm_codes[:, i, :].bitcast(E4M3), scales=wm_scales[:, i, :],
@@ -164,7 +189,7 @@ def tile_rwkv_timemix_for_quant_pa_v_kernel(
                 T["dx", i] = dx
             else:
                 t = step - 1
-                md = sb.tile([P, PACK, E // 2], F32, tag="md", name="md")
+                md = sb.tile([P, PACK, E // 2], F32, tag="md", name="md", bufs=1)
                 m = mix[:, t, eh * (E // 2):(eh + 1) * (E // 2)]
                 nc.gpsimd.tensor_tensor(md[:], T["dx", i][:], m.unsqueeze(1).broadcast_to([P, PACK, E // 2]), ALU.mult)
                 T["md", i, t] = md
@@ -172,7 +197,7 @@ def tile_rwkv_timemix_for_quant_pa_v_kernel(
         def x_add(i, t):
             g, eh = divmod(i, 2)
             if eh == 0:
-                T["xg", g, t] = grouped()
+                T["xg", g, t] = grouped("xg", 2)
             dst = T["xg", g, t][:, eh * (E // 2):(eh + 1) * (E // 2), :]
             nc.vector.tensor_tensor(dst, T["md", i, t][:].rearrange("p j e -> p e j"),
                                     T["sx", i][:].rearrange("p j e -> p e j"), ALU.add)
@@ -183,20 +208,24 @@ def tile_rwkv_timemix_for_quant_pa_v_kernel(
             nc.vector.quantize_mx(out=xm_codes[:, 2 * g + t, :].bitcast(E4M3), scales=xm_scales[:, 2 * g + t, :],
                                   in_=T["xg", g, t][:].rearrange("p e j -> p (e j)"))
 
-        def casts(u):
+        def casts(u, names=("sp", "sA", "sB")):
             if u >= UNITS:
                 return
-            for name, scale, bias in (("sp", -1.0, 0.0), ("sA", 1.0, 0.0), ("sB", -1.0, -1.0)):
+            for name in names:
+                scale, bias = {"sp": (-1.0, 0.0), "sA": (1.0, 0.0), "sB": (-1.0, -1.0)}[name]
                 c = sb.tile([P, PACK, P], F32, tag="c_" + name, name="c_" + name)
                 nc.scalar.activation(c[:], cols(name, u), ACT.Copy, bias=bias, scale=scale)
                 T["c_" + name, u] = c
-            release(u, "sp", "sA", "sB")
+            release(u, *names)
+
+        def has_gap(u, jobs):
+            return u >= 1 and all(job[0] == "y" for job in jobs.get(u, []))
 
         def fill_s(u):
             if u >= UNITS:
                 return
             s = bank("s", F32)
-            transpose_sum(s, [lambda j: cols("k", u)[:, j, :], lambda j: T["c_sp", u][:, j, :]])
+            transpose_sum(s, [lambda j: cols("k", u)[:, j, :], lambda j: T["c_sp", u][:, j, :]], warm=has_gap(u - 1, early) and "s" in PTS)
             T["s", u] = s
             release(u, "k")
 
@@ -225,13 +254,13 @@ def tile_rwkv_timemix_for_quant_pa_v_kernel(
                 return
             if what == "vA":
                 b = bank("fwd", F32)
-                transpose_sum(b, [lambda j: cols("v", u)[:, j, :], lambda j: T["c_sA", u][:, j, :]])
+                transpose_sum(b, [lambda j: cols("v", u)[:, j, :], lambda j: T["c_sA", u][:, j, :]], warm=u > 0 and "vA" in PTS)
             elif what == "nsB":
                 b = bank("fwd", F32)
-                transpose_sum(b, [lambda j: T["c_sB", u][:, j, :]])
+                transpose_sum(b, [lambda j: T["c_sB", u][:, j, :]], warm=u > 0 and "nsB" in PTS)
             elif what == "v":
                 b = bank("fwd", F32)
-                transpose_sum(b, [lambda j: cols("v", u)[:, j, :]])
+                transpose_sum(b, [lambda j: cols("v", u)[:, j, :]], warm=has_gap(u - 1, late) and "v" in PTS)
                 release(u, "v")
             else:
                 names = {"g13": ("g1", "g3"), "g02": ("g0", "g2"), "g4": ("g4",)}[what]
@@ -295,7 +324,7 @@ def tile_rwkv_timemix_for_quant_pa_v_kernel(
             else:
                 dvt = T["dvt", u]
                 terms = [lambda j: dvt[:, 0, j * P:(j + 1) * P], lambda j: dvt[:, 1, j * P:(j + 1) * P]]
-            transpose_sum(b, terms)
+            transpose_sum(b, terms, warm=(("dk", "dv")[t] in PTS and u < UNITS - 2))
             T["back", t, u] = b
 
         def x_copy(t, u):
@@ -340,13 +369,12 @@ def tile_rwkv_timemix_for_quant_pa_v_kernel(
                                 lhsT_scale=T[name + "s", c][:, lo:lo + P],
                                 rhs=codes[:, i, :].bitcast(E4M3), rhs_scale=scales[:, i, :], start=start, stop=stop)
 
-        def dx_passes(g, m, fgs, kind="back"):
+        def dx_passes(g, m, passes, kind="back"):
             if ("o0", g, m) not in T:
                 T["o0", g, m] = bank(kind, F32)
-            for fg in fgs:
-                for t in range(2):
-                    mx(T["o0", g, m], "yy", 2 * g + fg, t, m, wm_codes, wm_scales, 2 * t + fg,
-                       fg == 0 and t == 0, fg == 1 and t == 1)
+            for fg, t in passes:
+                mx(T["o0", g, m], "yy", 2 * g + fg, t, m, wm_codes, wm_scales, 2 * t + fg,
+                   (fg, t) == DX_ORDER[0], (fg, t) == DX_ORDER[-1])
 
         def dw_passes(t, fg, m, kind="back"):
             acc = bank(kind, F32)
@@ -355,7 +383,7 @@ def tile_rwkv_timemix_for_quant_pa_v_kernel(
             T["ow", t, fg, m] = acc
 
         def store(acc, dst, blk, m, eng="s"):
-            st = sb.tile([P, E], F32, tag="st", name="st", bufs=3)
+            st = sb.tile([P, E], F32, tag="st", name="st", bufs=8)
             if eng == "s":
                 nc.scalar.copy(st[:], acc[:])
             else:
@@ -367,7 +395,7 @@ def tile_rwkv_timemix_for_quant_pa_v_kernel(
             if job[0] == "y":
                 y_fill(*job[1:])
             elif job[0] == "dx":
-                dx_passes(job[1], job[2], (0, 1))
+                dx_passes(job[1], job[2], DX_ORDER)
             else:
                 dw_passes(*job[1:])
 
@@ -379,109 +407,143 @@ def tile_rwkv_timemix_for_quant_pa_v_kernel(
             else:
                 store(T["ow", job[1], job[2], job[3]], outs_w[job[1]], job[2], job[3])
 
-        early = {5: [("y", 0, 0, 0)], 6: [("y", 0, 0, 1)], 7: [("y", 0, 1, 0)], 8: [("y", 0, 1, 1)],
+        early = {5: [("y", 0, 0, 0)], 6: [("y", 0, 1, 0)],
                  9: [("y", 1, 0, 0)], 10: [("y", 1, 1, 0)], 12: [("dx", 0, 1)],
                  13: [("y", 2, 0, 0), ("y", 2, 0, 1)], 14: [("y", 2, 1, 0), ("y", 2, 1, 1)],
                  15: [("dw", 1, 0, 0), ("dw", 1, 0, 1)]}
-        late = {9: [("y", 1, 0, 1)], 10: [("y", 1, 1, 1)], 11: [("dx", 0, 0)], 12: [("dx", 0, 2), ("dx", 0, 3)],
+        late = {5: [("y", 0, 0, 1)], 6: [("y", 0, 1, 1)], 9: [("y", 1, 0, 1)], 10: [("y", 1, 1, 1)], 11: [("dx", 0, 0)],
+                12: [("dx", 0, 2), ("dx", 0, 3)],
                 13: [("dw", 0, 0, 0), ("dw", 0, 0, 1)], 14: [("dw", 0, 0, 2), ("dw", 0, 0, 3)],
                 15: [("dw", 1, 0, 2), ("dw", 1, 0, 3)]}
         vec_extra = {
-            0: [lambda: wm_quant(0)],
-            1: [lambda: x_add(0, 0)], 2: [lambda: x_add(0, 1)], 3: [lambda: wm_mult(1)],
-            4: [lambda: x_add(1, 0), lambda: wm_quant(1)],
-            5: [lambda: quant("xx", 0, (0, 1)), lambda: x_add(1, 1), lambda: x_quant(0, 0)],
-            6: [lambda: x_quant(0, 1), lambda: wm_mult(2)],
-            7: [lambda: x_add(2, 0), lambda: wm_quant(2)],
-            8: [lambda: x_add(2, 1), lambda: quant("yy", 0, (0, 1))],
-            9: [lambda: quant("xx", 1, (0, 1))],
-            10: [lambda: wm_mult(3), lambda: x_add(3, 0)],
-            11: [lambda: wm_quant(3), lambda: quant("yy", 1, (0, 1)), lambda: x_add(3, 1), lambda: x_quant(1, 0)],
-            12: [lambda: x_quant(1, 1)],
-            13: [lambda: quant("xx", 2, (0, 1))],
-            15: [lambda: quant("yy", 2, (0, 1))],
+            2: [lambda: wm_mult(1)],
+            3: [lambda: x_add(0, 0)],
+            5: [lambda: quant("xx", 0, (0, 1)), lambda: wm_quant(1), lambda: wm_mult(2), lambda: x_add(0, 1)],
+            6: [lambda: x_add(1, 0)],
+            8: [lambda: quant("yy", 0, (0, 1)), lambda: x_quant(0, 0), lambda: wm_quant(2), lambda: wm_mult(3),
+                lambda: x_add(1, 1)],
+            9: [lambda: quant("xx", 1, (0, 1)), lambda: x_quant(0, 1), lambda: wm_quant(3), lambda: x_add(2, 0)],
+            11: [lambda: quant("yy", 1, (0, 1)), lambda: x_add(2, 1)],
+            12: [lambda: x_add(3, 0)],
+            13: [lambda: quant("xx", 2, (0, 1)), lambda: x_quant(1, 0), lambda: x_add(3, 1)],
+            14: [lambda: x_quant(1, 1)],
         }
-        pool_extra = {u: [u + 1] for u in range(1, 11)}
-        pool_extra[0] = [0, 1]
+        act_extra = {3: 1, 7: 2, 8: 3}
+        pool_extra = {u: [u - 1] for u in range(1, 13)}
 
-        casts(0)
+        casts(0, ("sp",))
         fill_s(0)
+        casts(0, ("sA", "sB"))
+        wm_first()
+        load_w(1)
+        load_x(1)
         exps_read(0)
-        wm_mult(0)
         fill("vA", 0)
         fill("nsB", 0)
         fill("v", 0)
         casts(1)
         exps_rest(0)
         fill("g13", 0)
+        wm_quant(0)
+        nc.vector.quantize_mx(out=warm_codes[:].bitcast(E5M2), scales=warm_scales[:],
+                              in_=T["wg", 0][:].rearrange("q e j -> q (e j)")[:, 0:KP])
 
         last = UNITS - 1
-        for u in range(UNITS):
-            fill_s(u + 1)
+        for u in range(last):
             for job in early.get(u, []):
                 job_pe(job)
+                job_copy(job)
+            fill_s(u + 1)
             op_a(u)
             exps_read(u + 1)
             fill("g02", u)
             op_d(u)
             fill("g4", u)
-            for job in early.get(u, []):
-                job_copy(job)
-            exps_rest(u + 1)
             back(1, u - 1)
             x_copy(1, u - 1)
+            casts(u + 2)
             back(0, u - 1)
             x_copy(0, u - 1)
+            exps_rest(u + 1)
             op_b(u)
             fill("vA", u + 1)
             op_e(u)
             fill("nsB", u + 1)
-            for n in pool_extra.get(u, []):
-                x_piece(n)
             for job in vec_extra.get(u, []):
                 job()
+            for n in pool_extra.get(u, []):
+                x_piece(n)
             for job in late.get(u, []):
                 job_pe(job)
             op_c(u)
-            if u < last:
-                op_f(u, nc.gpsimd)
-                op_g(u, nc.gpsimd)
-            casts(u + 2)
+            op_f(u, nc.gpsimd)
+            op_g(u, nc.gpsimd)
             for job in late.get(u, []):
                 job_copy(job)
+            if u in act_extra:
+                wm_interleave(act_extra[u])
             op_h(u)
             fill("v", u + 1)
-            if u == last:
-                op_f(u, nc.vector)
             op_m(u)
             fill("g13", u + 1)
 
-        back(1, last)
+        op_a(last)
+        fill("g02", last)
+        op_d(last)
+        fill("g4", last)
+        back(1, last - 1)
+        x_copy(1, last - 1)
+        for job in early[last]:
+            job_pe(job)
+            job_copy(job)
+        op_h(last)
+        back(1, last, kind="s")
         x_copy(1, last)
-        op_g(last, nc.vector)
-        for m in range(4):
-            dx_passes(1, m, (0,), kind="fwd")
+        back(0, last - 1)
+        x_copy(0, last - 1)
+        op_b(last)
+        quant("yy", 2, (0, 1))
         y_fill(3, 1, 0)
         y_fill(3, 1, 1, kind="s")
+        op_e(last)
         quant("xx", 3, (1,))
-        back(0, last)
         y_copy(3, 1, 0)
+        y_copy(3, 1, 1)
+        for job in late[last]:
+            job_pe(job)
+            job_copy(job)
+        op_c(last)
+        op_m(last)
+        op_f(last, nc.vector)
+        for m in range(4):
+            dw_passes(1, 1, m, kind=("s" if m == 1 else "back"))
+            store(T["ow", 1, 1, m], out_2, 1, m)
+            dx_passes(1, m, DX_ORDER[:2], kind="fwd")
+        quant("yy", 3, (1,))
+        op_g(last, nc.vector)
+        back(0, last)
         x_copy(0, last)
-        y_copy(3, 1, 1, eng="v")
-        dw_passes(1, 1, 0)
-        dw_passes(1, 1, 1)
+        for m in range(2):
+            dx_passes(1, m, DX_ORDER[2:3])
         y_fill(3, 0, 0)
         y_fill(3, 0, 1, kind="s")
         quant("xx", 3, (0,))
         y_copy(3, 0, 0)
         y_copy(3, 0, 1, eng="v")
-        store(T["ow", 1, 1, 0], out_2, 1, 0)
-        store(T["ow", 1, 1, 1], out_2, 1, 1)
-        quant("yy", 3, (0, 1))
-        tiles = [(1, 2), (1, 3), (0, 0), (0, 1), (0, 2), (0, 3)]
-        for n, (t, m) in enumerate(tiles):
-            dw_passes(t, 1, m, kind=("s" if n % 4 == 3 else "back"))
-            store(T["ow", t, 1, m], outs_w[t], 1, m, eng=("s" if n % 2 == 0 else "v"))
+        for m in range(2):
+            dw_passes(0, 1, m)
+        for m in range(2, 4):
+            dx_passes(1, m, DX_ORDER[2:3])
+        quant("yy", 3, (0,))
+        for m in range(2):
+            store(T["ow", 0, 1, m], out_1, 1, m)
+        for m in range(2, 4):
+            dw_passes(0, 1, m, kind=("s" if m == 3 else "back"))
         for m in range(4):
-            dx_passes(1, m, (1,))
-            store(T["o0", 1, m], out_0, 1, m, eng=("s" if m % 2 == 0 else "v"))
+            dx_passes(1, m, DX_ORDER[3:])
+        order = [("ow", 2, "v"), ("ow", 3, "v"), ("o0", 0, "s"), ("o0", 1, "v"), ("o0", 2, "s"), ("o0", 3, "v")]
+        for kind, m, eng in order:
+            if kind == "ow":
+                store(T["ow", 0, 1, m], out_1, 1, m, eng=eng)
+            else:
+                store(T["o0", 1, m], out_0, 1, m, eng=eng)

@@ -20,7 +20,7 @@ PACK = 4
 KP = P * PACK
 UNITS = 16
 LOAD_W = 256
-WARM = 2
+WARM = 0
 PTS = ("s", "dk", "v")
 DX_ORDER = ((0, 0), (0, 1), (1, 1), (1, 0))
 
@@ -107,8 +107,8 @@ def tile_rwkv_timemix_for_quant_pa_v_kernel(
         wm_scales = keep.tile([P, 4, E], U8, align_bytes=64)
         xm_codes = keep.tile([P, 4, E], U32, align_bytes=64)
         xm_scales = keep.tile([P, 4, E], U8, align_bytes=64)
-        warm_codes = keep.tile([P, P], U32, align_bytes=64)
-        warm_scales = keep.tile([P, P], U8, align_bytes=64)
+        warm_codes = wm_codes
+        warm_scales = wm_scales
         colv = keep.tile([P, 24], F32)
         decay = keep.tile([P, 8], F32)
         mix = keep.tile([P, 2, E], BF16)
@@ -445,8 +445,6 @@ def tile_rwkv_timemix_for_quant_pa_v_kernel(
         exps_rest(0)
         fill("g13", 0)
         wm_quant(0)
-        nc.vector.quantize_mx(out=warm_codes[:].bitcast(E5M2), scales=warm_scales[:],
-                              in_=T["wg", 0][:].rearrange("q e j -> q (e j)")[:, 0:KP])
 
         last = UNITS - 1
         for u in range(last):

@@ -20,8 +20,10 @@ PACK = 4
 KP = P * PACK
 UNITS = 16
 LOAD_W = 256
-WARM = 0
+GCAST = ("sp", "sA", "sB")
 PTS = ("s", "dk", "v")
+WMS = True
+XPER = (2, 3, 4, 5, 7, 8, 11, 12)
 DX_ORDER = ((0, 0), (0, 1), (1, 1), (1, 0))
 
 
@@ -76,10 +78,6 @@ def tile_rwkv_timemix_for_quant_pa_v_kernel(
                     load(name, u // 2 + 2)
 
         def transpose_sum(dst, terms, warm=False):
-            for rep in range(WARM if warm else 0):
-                nc.tensor.matmul_mx(out=dst[:], lhsT=warm_codes[:].bitcast(E5M2), lhsT_scale=warm_scales[:],
-                                    rhs=wm_codes[:, 0, :].bitcast(E4M3), rhs_scale=wm_scales[:, 0, :],
-                                    start=True, stop=True)
             for j in range(PACK):
                 for i, term in enumerate(terms):
                     nc.tensor.matmul(dst[:, j * P:(j + 1) * P], lhsT=term(j), rhs=ident32[:], is_transpose=True,
@@ -107,8 +105,7 @@ def tile_rwkv_timemix_for_quant_pa_v_kernel(
         wm_scales = keep.tile([P, 4, E], U8, align_bytes=64)
         xm_codes = keep.tile([P, 4, E], U32, align_bytes=64)
         xm_scales = keep.tile([P, 4, E], U8, align_bytes=64)
-        warm_codes = wm_codes
-        warm_scales = wm_scales
+        rest = keep.tile([P, 8], F32)
         colv = keep.tile([P, 24], F32)
         decay = keep.tile([P, 8], F32)
         mix = keep.tile([P, 2, E], BF16)
@@ -140,9 +137,9 @@ def tile_rwkv_timemix_for_quant_pa_v_kernel(
             load(name, 0, P, LOAD_W)
         for name in ("sp", "k", "sA", "v", "sB"):
             load(name, 1)
-        load_x(0)
         for name in ("g1", "g3", "g0", "g2", "g4"):
             load(name, 1)
+        load_x(0)
 
         small = bank("back", BF16)
         nc.tensor.transpose(small[:, 0:P], rows[:], ident16[:])
@@ -164,6 +161,13 @@ def tile_rwkv_timemix_for_quant_pa_v_kernel(
                                     mix[:, 0, :].unsqueeze(2).broadcast_to([P, E, PACK]), ALU.mult)
 
         def wm_mult(i):
+            if not WMS:
+                T["wg", i] = grouped("wg", 1)
+                nc.vector.tensor_tensor(T["wg", i][:], T["w", i][:].rearrange("q j e -> q e j"),
+                                        mix[:, i // 2, :].unsqueeze(2).broadcast_to([P, E, PACK]), ALU.mult)
+                if i + 1 < 4:
+                    load_w(i + 1)
+                return
             wp = sb.tile([P, PACK, E], BF16, tag="wp", name="wp", bufs=1)
             nc.vector.tensor_tensor(wp[:], T["w", i][:], mix[:, i // 2, :].unsqueeze(1).broadcast_to([P, PACK, E]),
                                     ALU.mult)
@@ -172,6 +176,8 @@ def tile_rwkv_timemix_for_quant_pa_v_kernel(
                 load_w(i + 1)
 
         def wm_interleave(i):
+            if not WMS:
+                return
             T["wg", i] = grouped("wg", 1)
             nc.scalar.copy(T["wg", i][:].rearrange("q (c i) j -> q c j i", i=4),
                            T["wp", i][:].rearrange("q j (c i) -> q c j i", i=4))
@@ -180,29 +186,41 @@ def tile_rwkv_timemix_for_quant_pa_v_kernel(
             nc.vector.quantize_mx(out=wm_codes[:, i, :].bitcast(E4M3), scales=wm_scales[:, i, :],
                                   in_=T["wg", i][:].rearrange("q e j -> q (e j)"))
 
-        def x_piece(n):
-            i, step = divmod(n, 3)
-            eh = i % 2
-            if step == 0:
-                dx = sb.tile([P, PACK, E // 2], F32, tag="dx", name="dx", bufs=1)
-                nc.gpsimd.tensor_tensor(dx[:], T["x", i][:], T["sx", i][:], ALU.subtract)
-                T["dx", i] = dx
-            else:
-                t = step - 1
-                md = sb.tile([P, PACK, E // 2], F32, tag="md", name="md", bufs=1)
-                m = mix[:, t, eh * (E // 2):(eh + 1) * (E // 2)]
-                nc.gpsimd.tensor_tensor(md[:], T["dx", i][:], m.unsqueeze(1).broadcast_to([P, PACK, E // 2]), ALU.mult)
-                T["md", i, t] = md
+        def mix_columns():
+            nc.scalar.activation(rest[:], colv[:, 16:24], ACT.Copy, bias=1.0, scale=-1.0)
 
-        def x_add(i, t):
-            g, eh = divmod(i, 2)
-            if eh == 0:
+        def x_turn(i):
+            b = bank("back", BF16)
+            for h, name in enumerate(("x", "sx")):
+                for j in range(PACK):
+                    nc.tensor.transpose(b[:, h * KP + j * P:h * KP + (j + 1) * P],
+                                        T[name, i // 2][:, j, (i % 2) * P:(i % 2 + 1) * P], ident16[:])
+            T["xT", i] = b
+            if i % 2 == 1 and i // 2 + 2 < 4:
+                load_x(i // 2 + 2)
+
+        def x_scale(i):
+            part = sb.tile([P, 4, KP], F32, tag="xpart", name="xpart", bufs=1)
+            for t in range(2):
+                col = 4 * t + i % 4
+                for h, factor in enumerate((colv[:, 16 + col:17 + col], rest[:, col:col + 1])):
+                    nc.scalar.activation(part[:, 2 * t + h, :], T["xT", i][:, h * KP:(h + 1) * KP], ACT.Copy,
+                                         scale=factor)
+            T["xpart", i] = part
+
+        def x_back(i, t):
+            b = bank("back", F32)
+            part = T["xpart", i]
+            transpose_sum(b, [lambda j: part[:, 2 * t, j * P:(j + 1) * P],
+                              lambda j: part[:, 2 * t + 1, j * P:(j + 1) * P]])
+            T["xb", i, t] = b
+
+        def x_back_copy(i, t):
+            g, eb = divmod(i, 4)
+            if eb == 0:
                 T["xg", g, t] = grouped("xg", 2)
-            dst = T["xg", g, t][:, eh * (E // 2):(eh + 1) * (E // 2), :]
-            nc.vector.tensor_tensor(dst, T["md", i, t][:].rearrange("p j e -> p e j"),
-                                    T["sx", i][:].rearrange("p j e -> p e j"), ALU.add)
-            if t == 1 and i + 2 < 4:
-                load_x(i + 2)
+            nc.scalar.copy(T["xg", g, t][:, eb * P:(eb + 1) * P, :],
+                           T["xb", i, t][:].rearrange("p (j e) -> p e j", j=PACK))
 
         def x_quant(g, t):
             nc.vector.quantize_mx(out=xm_codes[:, 2 * g + t, :].bitcast(E4M3), scales=xm_scales[:, 2 * g + t, :],
@@ -214,7 +232,10 @@ def tile_rwkv_timemix_for_quant_pa_v_kernel(
             for name in names:
                 scale, bias = {"sp": (-1.0, 0.0), "sA": (1.0, 0.0), "sB": (-1.0, -1.0)}[name]
                 c = sb.tile([P, PACK, P], F32, tag="c_" + name, name="c_" + name)
-                nc.scalar.activation(c[:], cols(name, u), ACT.Copy, bias=bias, scale=scale)
+                if name in GCAST and u > 2:
+                    nc.gpsimd.tensor_scalar(c[:], cols(name, u), scale, bias, ALU.mult, ALU.add)
+                else:
+                    nc.scalar.activation(c[:], cols(name, u), ACT.Copy, bias=bias, scale=scale)
                 T["c_" + name, u] = c
             release(u, *names)
 
@@ -392,7 +413,11 @@ def tile_rwkv_timemix_for_quant_pa_v_kernel(
                               in_=st[:])
 
         def job_pe(job):
-            if job[0] == "y":
+            if job[0] == "xt":
+                x_turn(job[1])
+            elif job[0] == "xb":
+                x_back(*job[1:])
+            elif job[0] == "y":
                 y_fill(*job[1:])
             elif job[0] == "dx":
                 dx_passes(job[1], job[2], DX_ORDER)
@@ -400,7 +425,11 @@ def tile_rwkv_timemix_for_quant_pa_v_kernel(
                 dw_passes(*job[1:])
 
         def job_copy(job):
-            if job[0] == "y":
+            if job[0] == "xt":
+                x_scale(job[1])
+            elif job[0] == "xb":
+                x_back_copy(*job[1:])
+            elif job[0] == "y":
                 y_copy(*job[1:])
             elif job[0] == "dx":
                 store(T["o0", job[1], job[2]], out_0, job[1], job[2])
@@ -415,21 +444,20 @@ def tile_rwkv_timemix_for_quant_pa_v_kernel(
                 12: [("dx", 0, 2), ("dx", 0, 3)],
                 13: [("dw", 0, 0, 0), ("dw", 0, 0, 1)], 14: [("dw", 0, 0, 2), ("dw", 0, 0, 3)],
                 15: [("dw", 1, 0, 2), ("dw", 1, 0, 3)]}
+        for i, u in enumerate(XPER):
+            early[u] = [("xt", i)] + early.get(u, [])
+            late[u] = [("xb", i, 0), ("xb", i, 1)] + late.get(u, [])
         vec_extra = {
-            2: [lambda: wm_mult(1)],
-            3: [lambda: x_add(0, 0)],
-            5: [lambda: quant("xx", 0, (0, 1)), lambda: wm_quant(1), lambda: wm_mult(2), lambda: x_add(0, 1)],
-            6: [lambda: x_add(1, 0)],
-            8: [lambda: quant("yy", 0, (0, 1)), lambda: x_quant(0, 0), lambda: wm_quant(2), lambda: wm_mult(3),
-                lambda: x_add(1, 1)],
-            9: [lambda: quant("xx", 1, (0, 1)), lambda: x_quant(0, 1), lambda: wm_quant(3), lambda: x_add(2, 0)],
-            11: [lambda: quant("yy", 1, (0, 1)), lambda: x_add(2, 1)],
-            12: [lambda: x_add(3, 0)],
-            13: [lambda: quant("xx", 2, (0, 1)), lambda: x_quant(1, 0), lambda: x_add(3, 1)],
-            14: [lambda: x_quant(1, 1)],
+            4: [lambda: wm_mult(1)],
+            5: [lambda: quant("xx", 0, (0, 1))],
+            6: [lambda: x_quant(0, 0), lambda: x_quant(0, 1), lambda: wm_quant(1), lambda: wm_mult(2)],
+            7: [lambda: quant("yy", 0, (0, 1)), lambda: wm_quant(2)],
+            9: [lambda: quant("xx", 1, (0, 1)), lambda: wm_mult(3)],
+            10: [lambda: wm_quant(3)],
+            11: [lambda: quant("yy", 1, (0, 1))],
+            13: [lambda: quant("xx", 2, (0, 1)), lambda: x_quant(1, 0), lambda: x_quant(1, 1)],
         }
-        act_extra = {3: 1, 7: 2, 8: 3}
-        pool_extra = {u: [u - 1] for u in range(1, 13)}
+        act_extra = {5: 1, 6: 2, 9: 3}
 
         casts(0, ("sp",))
         fill_s(0)
@@ -445,6 +473,7 @@ def tile_rwkv_timemix_for_quant_pa_v_kernel(
         exps_rest(0)
         fill("g13", 0)
         wm_quant(0)
+        mix_columns()
 
         last = UNITS - 1
         for u in range(last):
@@ -469,8 +498,6 @@ def tile_rwkv_timemix_for_quant_pa_v_kernel(
             fill("nsB", u + 1)
             for job in vec_extra.get(u, []):
                 job()
-            for n in pool_extra.get(u, []):
-                x_piece(n)
             for job in late.get(u, []):
                 job_pe(job)
             op_c(u)

from contextlib import ExitStack

import concourse.mybir as mybir
from concourse.masks import make_identity

B, E, D = 1024, 512, 1024
FLOPS = 2 * B * 2 * D * E + 2 * 2 * B * D * E

F32 = mybir.dt.float32
BF16 = mybir.dt.bfloat16
U32 = mybir.dt.uint32
U8 = mybir.dt.uint8
E4M3 = mybir.dt.float8_e4m3fn_x4
E5M2 = mybir.dt.float8_e5m2_x4
ALU = mybir.AluOpType
ACT = mybir.ActivationFunctionType

P = 128
PACK = 4
KP = P * PACK
UNITS = 16
LOAD_W = 256
GCAST = ("sp", "sA", "sB")
PTS = ("s", "dk", "v")
WMS = True
XPER = (2, 3, 4, 5, 7, 8, 11, 12)
DX_ORDER = ((0, 0), (0, 1), (1, 1), (1, 0))


def tile_rwkv_timemix_for_quant_pa_v_kernel(
    tc, x, state_A, state_B, state_p, state_x, time_decay, time_first, time_mix_k, time_mix_v,
    W_key, W_value, k, v, grad_0, grad_1, grad_2, grad_3, grad_4, out_0, out_1, out_2,
):
    nc = tc.nc
    src = {"k": k, "sp": state_p, "sA": state_A, "v": v, "sB": state_B,
           "g1": grad_1, "g3": grad_3, "g0": grad_0, "g2": grad_2, "g4": grad_4}
    weights = (W_key, W_value)
    outs_w = (out_1, out_2)

    with ExitStack() as ctx:
        keep = ctx.enter_context(tc.tile_pool(name="keep", bufs=1))
        sb = ctx.enter_context(tc.tile_pool(name="sb", bufs=2))
        ps = ctx.enter_context(tc.psum_pool(name="ps", bufs=1))
        ctx.enter_context(tc.manual_schedule())

        loaded = {}
        T = {}
        count = {"fwd": 0, "back": 0}

        def bank(kind, dtype):
            if kind == "fwd":
                tag = "fwd%d" % (count["fwd"] % 4)
                count["fwd"] = count["fwd"] + 1
            elif kind == "back":
                tag = "back%d" % (count["back"] % 3)
                count["back"] = count["back"] + 1
            else:
                tag = kind
            width = KP if dtype == F32 else 2 * KP
            return ps.tile([P, width], dtype, tag=tag, name=tag)

        def load(name, sc, lo=0, hi=LOAD_W):
            if sc >= UNITS // 2:
                return
            g, q = divmod(sc, 4)
            if lo == 0:
                loaded[name, sc] = sb.tile([P, PACK, LOAD_W], src[name].dtype, tag="in_" + name, name="in_" + name)
            rows = src[name][g * KP:(g + 1) * KP, q * LOAD_W + lo:q * LOAD_W + hi]
            nc.sync.dma_start(out=loaded[name, sc][:, :, lo:hi], in_=rows.rearrange("(p j) w -> p j w", j=PACK))

        def cols(name, u):
            h = u % 2
            return loaded[name, u // 2][:, :, h * P:(h + 1) * P]

        def release(u, *names):
            if u % 2 == 1:
                for name in names:
                    load(name, u // 2 + 2)

        def transpose_sum(dst, terms, warm=False):
            for j in range(PACK):
                for i, term in enumerate(terms):
                    nc.tensor.matmul(dst[:, j * P:(j + 1) * P], lhsT=term(j), rhs=ident32[:], is_transpose=True,
                                     start=(i == 0), stop=(i == len(terms) - 1))

        def transpose_bf16(dst, name, u):
            for j in range(PACK):
                nc.tensor.transpose(dst[:, j * P:(j + 1) * P], cols(name, u)[:, j, :], ident16[:])

        def twice(ap):
            return ap.unsqueeze(1).broadcast_to([P, 2, KP])

        rows = keep.tile([P, P], BF16)
        nc.vector.memset(rows[:], 0.0)
        nc.sync.dma_start(out=rows[0:8, :], in_=time_first.rearrange("(c p) -> c p", p=P))
        nc.sync.dma_start(out=rows[8:16, :], in_=time_decay.rearrange("(c p) -> c p", p=P))
        nc.sync.dma_start(out=rows[16:20, :], in_=time_mix_k.rearrange("o (c p) -> (o c) p", p=P))
        nc.sync.dma_start(out=rows[20:24, :], in_=time_mix_v.rearrange("o (c p) -> (o c) p", p=P))
        ident16 = keep.tile([P, P], BF16)
        ident32 = keep.tile([P, P], F32)
        make_identity(nc, ident16[:])
        make_identity(nc, ident32[:])

        wm_codes = keep.tile([P, 4, E], U32, align_bytes=64)
        wm_scales = keep.tile([P, 4, E], U8, align_bytes=64)
        xm_codes = keep.tile([P, 4, E], U32, align_bytes=64)
        xm_scales = keep.tile([P, 4, E], U8, align_bytes=64)
        rest = keep.tile([P, 8], F32)
        colv = keep.tile([P, 24], F32)
        decay = keep.tile([P, 8], F32)
        mix = keep.tile([P, 2, E], BF16)

        def load_w(i):
            t, fg = divmod(i, 2)
            w = sb.tile([P, PACK, E], BF16, tag="w_raw", name="w_raw", bufs=1)
            nc.sync.dma_start(out=w[:], in_=weights[t][fg * KP:(fg + 1) * KP, :].rearrange("(q j) e -> q j e", j=PACK))
            T["w", i] = w

        def load_x(i):
            g, eh = divmod(i, 2)
            for name, a in (("x", x), ("sx", state_x)):
                t = sb.tile([P, PACK, E // 2], BF16, tag=name, name=name)
                part = a[g * KP:(g + 1) * KP, eh * (E // 2):(eh + 1) * (E // 2)]
                nc.sync.dma_start(out=t[:], in_=part.rearrange("(p j) w -> p j w", j=PACK))
                T[name, i] = t

        load("k", 0, 0, P)
        load("sp", 0, 0, P)
        load_w(0)
        for name in ("sA", "v", "sB", "g1", "g3"):
            load(name, 0, 0, P)
        for name in ("sp", "k"):
            load(name, 0, P, LOAD_W)
        for name in ("g0", "g2", "g4"):
            load(name, 0, 0, P)
        for name in ("sA", "v", "sB", "g1", "g3", "g0", "g2", "g4"):
            load(name, 0, P, LOAD_W)
        for name in ("sp", "k", "sA", "v", "sB"):
            load(name, 1)
        for name in ("g1", "g3", "g0", "g2", "g4"):
            load(name, 1)
        load_x(0)

        small = bank("back", BF16)
        nc.tensor.transpose(small[:, 0:P], rows[:], ident16[:])
        nc.scalar.activation(decay[:], small[:, 8:16], ACT.Exp)
        nc.scalar.copy(colv[:], small[:, 0:24])
        for t in range(2):
            spread = bank("back", F32)
            for c in range(4):
                col = colv[:, 16 + 4 * t + c:17 + 4 * t + c]
                nc.tensor.transpose(spread[:, c * P:(c + 1) * P], col.to_broadcast([P, P]), ident32[:])
            nc.vector.tensor_copy(mix[:, t, :], spread[:])

        def grouped(tag, bufs):
            return sb.tile([P, E, PACK], BF16, tag=tag, name=tag, bufs=bufs, align_bytes=64)

        def wm_first():
            T["wg", 0] = grouped("wg", 1)
            nc.vector.tensor_tensor(T["wg", 0][:], T["w", 0][:].rearrange("q j e -> q e j"),
                                    mix[:, 0, :].unsqueeze(2).broadcast_to([P, E, PACK]), ALU.mult)

        def wm_mult(i):
            if not WMS:
                T["wg", i] = grouped("wg", 1)
                nc.vector.tensor_tensor(T["wg", i][:], T["w", i][:].rearrange("q j e -> q e j"),
                                        mix[:, i // 2, :].unsqueeze(2).broadcast_to([P, E, PACK]), ALU.mult)
                if i + 1 < 4:
                    load_w(i + 1)
                return
            wp = sb.tile([P, PACK, E], BF16, tag="wp", name="wp", bufs=1)
            nc.vector.tensor_tensor(wp[:], T["w", i][:], mix[:, i // 2, :].unsqueeze(1).broadcast_to([P, PACK, E]),
                                    ALU.mult)
            T["wp", i] = wp
            if i + 1 < 4:
                load_w(i + 1)

        def wm_interleave(i):
            if not WMS:
                return
            T["wg", i] = grouped("wg", 1)
            nc.scalar.copy(T["wg", i][:].rearrange("q (c i) j -> q c j i", i=4),
                           T["wp", i][:].rearrange("q j (c i) -> q c j i", i=4))

        def wm_quant(i):
            nc.vector.quantize_mx(out=wm_codes[:, i, :].bitcast(E4M3), scales=wm_scales[:, i, :],
                                  in_=T["wg", i][:].rearrange("q e j -> q (e j)"))

        def mix_columns():
            nc.scalar.activation(rest[:], colv[:, 16:24], ACT.Copy, bias=1.0, scale=-1.0)

        def x_turn(i):
            b = bank("back", BF16)
            for h, name in enumerate(("x", "sx")):
                for j in range(PACK):
                    nc.tensor.transpose(b[:, h * KP + j * P:h * KP + (j + 1) * P],
                                        T[name, i // 2][:, j, (i % 2) * P:(i % 2 + 1) * P], ident16[:])
            T["xT", i] = b
            if i % 2 == 1 and i // 2 + 2 < 4:
                load_x(i // 2 + 2)

        def x_scale(i):
            part = sb.tile([P, 4, KP], F32, tag="xpart", name="xpart", bufs=1)
            for t in range(2):
                col = 4 * t + i % 4
                for h, factor in enumerate((colv[:, 16 + col:17 + col], rest[:, col:col + 1])):
                    nc.scalar.activation(part[:, 2 * t + h, :], T["xT", i][:, h * KP:(h + 1) * KP], ACT.Copy,
                                         scale=factor)
            T["xpart", i] = part

        def x_back(i, t):
            b = bank("back", F32)
            part = T["xpart", i]
            transpose_sum(b, [lambda j: part[:, 2 * t, j * P:(j + 1) * P],
                              lambda j: part[:, 2 * t + 1, j * P:(j + 1) * P]])
            T["xb", i, t] = b

        def x_back_copy(i, t):
            g, eb = divmod(i, 4)
            if eb == 0:
                T["xg", g, t] = grouped("xg", 2)
            nc.scalar.copy(T["xg", g, t][:, eb * P:(eb + 1) * P, :],
                           T["xb", i, t][:].rearrange("p (j e) -> p e j", j=PACK))

        def x_quant(g, t):
            nc.vector.quantize_mx(out=xm_codes[:, 2 * g + t, :].bitcast(E4M3), scales=xm_scales[:, 2 * g + t, :],
                                  in_=T["xg", g, t][:].rearrange("p e j -> p (e j)"))

        def casts(u, names=("sp", "sA", "sB")):
            if u >= UNITS:
                return
            for name in names:
                scale, bias = {"sp": (-1.0, 0.0), "sA": (1.0, 0.0), "sB": (-1.0, -1.0)}[name]
                c = sb.tile([P, PACK, P], F32, tag="c_" + name, name="c_" + name)
                if name in GCAST and u > 2:
                    nc.gpsimd.tensor_scalar(c[:], cols(name, u), scale, bias, ALU.mult, ALU.add)
                else:
                    nc.scalar.activation(c[:], cols(name, u), ACT.Copy, bias=bias, scale=scale)
                T["c_" + name, u] = c
            release(u, *names)

        def has_gap(u, jobs):
            return u >= 1 and all(job[0] == "y" for job in jobs.get(u, []))

        def fill_s(u):
            if u >= UNITS:
                return
            s = bank("s", F32)
            transpose_sum(s, [lambda j: cols("k", u)[:, j, :], lambda j: T["c_sp", u][:, j, :]], warm=has_gap(u - 1, early) and "s" in PTS)
            T["s", u] = s
            release(u, "k")

        def exps_read(u):
            if u >= UNITS:
                return
            fb = u % 8
            bias = (colv[:, fb:fb + 1], decay[:, fb:fb + 1])
            xe = sb.tile([P, 2, KP], F32, tag="xe", name="xe")
            ee = sb.tile([P, 2, KP], F32, tag="ee", name="ee", bufs=3)
            for h in range(2):
                nc.scalar.activation(xe[:, h, :], T["s", u][:], ACT.Exp, bias=bias[h])
            for h in range(2):
                nc.scalar.activation(ee[:, h, :], T["s", u][:], ACT.Abs, bias=bias[h])
            T["xe", u] = xe
            T["ee", u] = ee

        def exps_rest(u):
            if u >= UNITS:
                return
            ee = T["ee", u]
            nc.scalar.activation(ee[:], ee[:], ACT.Exp, scale=-1.0)

        def fill(what, u):
            if u >= UNITS:
                return
            if what == "vA":
                b = bank("fwd", F32)
                transpose_sum(b, [lambda j: cols("v", u)[:, j, :], lambda j: T["c_sA", u][:, j, :]], warm=u > 0 and "vA" in PTS)
            elif what == "nsB":
                b = bank("fwd", F32)
                transpose_sum(b, [lambda j: T["c_sB", u][:, j, :]], warm=u > 0 and "nsB" in PTS)
            elif what == "v":
                b = bank("fwd", F32)
                transpose_sum(b, [lambda j: cols("v", u)[:, j, :]], warm=has_gap(u - 1, late) and "v" in PTS)
                release(u, "v")
            else:
                names = {"g13": ("g1", "g3"), "g02": ("g0", "g2"), "g4": ("g4",)}[what]
                b = bank("fwd", BF16)
                for h, name in enumerate(names):
                    transpose_bf16(b[:, h * KP:(h + 1) * KP], name, u)
                release(u, *names)
            T[what, u] = b

        def pair(ap):
            return ap.rearrange("p (h n) -> p h n", h=2)

        def op_a(u):
            a = sb.tile([P, 2, KP], F32, tag="a", name="a")
            nc.vector.scalar_tensor_tensor(a[:], T["xe", u][:], 1.0, twice(T["vA", u][:]), ALU.is_gt, ALU.mult)
            T["a", u] = a

        def op_d(u):
            b = sb.tile([P, 2, KP], F32, tag="b", name="b")
            nc.vector.scalar_tensor_tensor(b[:], T["xe", u][:], 1.0, twice(T["nsB", u][:]), ALU.is_gt, ALU.mult)
            T["b", u] = b

        def op_b(u):
            a = T["a", u]
            nc.vector.tensor_tensor(a[:], twice(T["v", u][:]), a[:], ALU.subtract)

        def op_e(u):
            b = T["b", u]
            nc.vector.scalar_tensor_tensor(b[:], b[:], 1.0, pair(T["g13", u][:]), ALU.add, ALU.mult)

        def op_c(u):
            a = T["a", u]
            nc.vector.tensor_tensor(a[:], pair(T["g02", u][:]), a[:], ALU.mult)

        def op_f(u, eng):
            a = T["a", u]
            eng.tensor_tensor(a[:], a[:], T["b", u][:], ALU.add)

        def op_g(u, eng):
            a = T["a", u]
            eng.tensor_tensor(a[:], a[:], T["ee", u][:], ALU.mult)

        def op_h(u):
            dvt = sb.tile([P, 2, KP], F32, tag="dvt", name="dvt")
            nc.vector.scalar_tensor_tensor(dvt[:], T["xe", u][:], 1.0, pair(T["g02", u][:]), ALU.min, ALU.mult)
            T["dvt", u] = dvt

        def op_m(u):
            mg = sb.tile([P, KP], F32, tag="mg", name="mg")
            nc.vector.scalar_tensor_tensor(mg[:], T["xe", u][:, 1, :], 1.0, T["g4", u][:, 0:KP], ALU.is_gt, ALU.mult)
            T["mg", u] = mg

        def back(t, u, kind="back"):
            if u < 0:
                return
            b = bank(kind, F32)
            if t == 0:
                a, mg = T["a", u], T["mg", u]
                terms = [lambda j: mg[:, j * P:(j + 1) * P], lambda j: a[:, 0, j * P:(j + 1) * P],
                         lambda j: a[:, 1, j * P:(j + 1) * P]]
            else:
                dvt = T["dvt", u]
                terms = [lambda j: dvt[:, 0, j * P:(j + 1) * P], lambda j: dvt[:, 1, j * P:(j + 1) * P]]
            transpose_sum(b, terms, warm=(("dk", "dv")[t] in PTS and u < UNITS - 2))
            T["back", t, u] = b

        def x_copy(t, u):
            if u < 0:
                return
            c, fbl = divmod(u, 4)
            if ("xx", c) not in T:
                T["xx", c] = sb.tile([P, 2, KP * PACK], BF16, tag="xx", name="xx", align_bytes=64)
            dst = T["xx", c][:, t, :].rearrange("p (jp f q j) -> p jp f q j", jp=PACK, f=4, j=PACK)[:, :, fbl, :, :]
            nc.scalar.copy(dst, T["back", t, u][:].rearrange("p (j q jp) -> p jp q j", j=PACK, jp=PACK))

        def quant(name, c, ts):
            if (name + "c", c) not in T:
                nb = 3 if name == "xx" else 2
                T[name + "c", c] = sb.tile([P, 2 * KP], U32, tag=name + "c", name=name + "c", bufs=nb, align_bytes=64)
                T[name + "s", c] = sb.tile([P, 2 * KP], U8, tag=name + "s", name=name + "s", bufs=nb, align_bytes=64)
            lo, hi = ts[0], ts[-1] + 1
            nc.vector.quantize_mx(out=T[name + "c", c][:, lo * KP:hi * KP].bitcast(E5M2),
                                  scales=T[name + "s", c][:, lo * KP:hi * KP],
                                  in_=T[name, c][:].rearrange("p t n -> p (t n)")[:, lo * KP * PACK:hi * KP * PACK])

        def y_fill(c, t, w, kind="back"):
            b = bank(kind, F32)
            words = T["xx", c][:, t, :].bitcast(F32)
            for jp in range(PACK):
                nc.tensor.transpose(b[:, jp * P:(jp + 1) * P], words[:, 2 * P * jp + w:2 * P * (jp + 1):2], ident32[:])
            T["yb", c, t, w] = b

        def y_copy(c, t, w, eng="s"):
            if ("yy", c) not in T:
                T["yy", c] = sb.tile([P, 2, KP * PACK], BF16, tag="yy", name="yy", bufs=1, align_bytes=64)
            dst = T["yy", c][:, t, w * 2 * KP:(w + 1) * 2 * KP].rearrange("q (e p jp) -> q e p jp", e=2, jp=PACK)
            s = T["yb", c, t, w][:].bitcast(BF16).rearrange("q (jp p e) -> q e p jp", jp=PACK, e=2)
            if eng == "s":
                nc.scalar.copy(dst, s)
            else:
                nc.vector.tensor_copy(dst, s)

        def mx(acc, name, c, t, m, codes, scales, i, start, stop):
            lo = t * KP + m * P
            nc.tensor.matmul_mx(out=acc[:], lhsT=T[name + "c", c][:, lo:lo + P].bitcast(E5M2),
                                lhsT_scale=T[name + "s", c][:, lo:lo + P],
                                rhs=codes[:, i, :].bitcast(E4M3), rhs_scale=scales[:, i, :], start=start, stop=stop)

        def dx_passes(g, m, passes, kind="back"):
            if ("o0", g, m) not in T:
                T["o0", g, m] = bank(kind, F32)
            for fg, t in passes:
                mx(T["o0", g, m], "yy", 2 * g + fg, t, m, wm_codes, wm_scales, 2 * t + fg,
                   (fg, t) == DX_ORDER[0], (fg, t) == DX_ORDER[-1])

        def dw_passes(t, fg, m, kind="back"):
            acc = bank(kind, F32)
            for g in range(2):
                mx(acc, "xx", 2 * g + fg, t, m, xm_codes, xm_scales, 2 * g + t, g == 0, g == 1)
            T["ow", t, fg, m] = acc

        def store(acc, dst, blk, m, eng="s"):
            st = sb.tile([P, E], F32, tag="st", name="st", bufs=8)
            if eng == "s":
                nc.scalar.copy(st[:], acc[:])
            else:
                nc.vector.tensor_copy(st[:], acc[:])
            nc.sync.dma_start(out=dst[blk * KP:(blk + 1) * KP, :].rearrange("(p j) e -> p j e", j=PACK)[:, m, :],
                              in_=st[:])

        def job_pe(job):
            if job[0] == "xt":
                x_turn(job[1])
            elif job[0] == "xb":
                x_back(*job[1:])
            elif job[0] == "y":
                y_fill(*job[1:])
            elif job[0] == "dx":
                dx_passes(job[1], job[2], DX_ORDER)
            else:
                dw_passes(*job[1:])

        def job_copy(job):
            if job[0] == "xt":
                x_scale(job[1])
            elif job[0] == "xb":
                x_back_copy(*job[1:])
            elif job[0] == "y":
                y_copy(*job[1:])
            elif job[0] == "dx":
                store(T["o0", job[1], job[2]], out_0, job[1], job[2])
            else:
                store(T["ow", job[1], job[2], job[3]], outs_w[job[1]], job[2], job[3])

        early = {5: [("y", 0, 0, 0)], 6: [("y", 0, 1, 0)],
                 9: [("y", 1, 0, 0)], 10: [("y", 1, 1, 0)], 12: [("dx", 0, 1)],
                 13: [("y", 2, 0, 0), ("y", 2, 0, 1)], 14: [("y", 2, 1, 0), ("y", 2, 1, 1)],
                 15: [("dw", 1, 0, 0), ("dw", 1, 0, 1)]}
        late = {5: [("y", 0, 0, 1)], 6: [("y", 0, 1, 1)], 9: [("y", 1, 0, 1)], 10: [("y", 1, 1, 1)], 11: [("dx", 0, 0)],
                12: [("dx", 0, 2), ("dx", 0, 3)],
                13: [("dw", 0, 0, 0), ("dw", 0, 0, 1)], 14: [("dw", 0, 0, 2), ("dw", 0, 0, 3)],
                15: [("dw", 1, 0, 2), ("dw", 1, 0, 3)]}
        for i, u in enumerate(XPER):
            early[u] = [("xt", i)] + early.get(u, [])
            late[u] = [("xb", i, 0), ("xb", i, 1)] + late.get(u, [])
        vec_extra = {
            4: [lambda: wm_mult(1)],
            5: [lambda: quant("xx", 0, (0, 1))],
            6: [lambda: x_quant(0, 0), lambda: x_quant(0, 1), lambda: wm_quant(1), lambda: wm_mult(2)],
            7: [lambda: quant("yy", 0, (0, 1)), lambda: wm_quant(2)],
            9: [lambda: quant("xx", 1, (0, 1)), lambda: wm_mult(3)],
            10: [lambda: wm_quant(3)],
            11: [lambda: quant("yy", 1, (0, 1))],
            13: [lambda: quant("xx", 2, (0, 1)), lambda: x_quant(1, 0), lambda: x_quant(1, 1)],
        }
        act_extra = {5: 1, 6: 2, 9: 3}

        casts(0, ("sp",))
        fill_s(0)
        casts(0, ("sA", "sB"))
        wm_first()
        load_w(1)
        load_x(1)
        exps_read(0)
        fill("vA", 0)
        fill("nsB", 0)
        fill("v", 0)
        casts(1)
        exps_rest(0)
        fill("g13", 0)
        wm_quant(0)
        mix_columns()

        last = UNITS - 1
        for u in range(last):
            for job in early.get(u, []):
                job_pe(job)
                job_copy(job)
            fill_s(u + 1)
            op_a(u)
            exps_read(u + 1)
            fill("g02", u)
            op_d(u)
            fill("g4", u)
            back(1, u - 1)
            x_copy(1, u - 1)
            casts(u + 2)
            back(0, u - 1)
            x_copy(0, u - 1)
            exps_rest(u + 1)
            op_b(u)
            fill("vA", u + 1)
            op_e(u)
            fill("nsB", u + 1)
            for job in vec_extra.get(u, []):
                job()
            for job in late.get(u, []):
                job_pe(job)
            op_c(u)
            op_f(u, nc.gpsimd)
            op_g(u, nc.gpsimd)
            for job in late.get(u, []):
                job_copy(job)
            if u in act_extra:
                wm_interleave(act_extra[u])
            op_h(u)
            fill("v", u + 1)
            op_m(u)
            fill("g13", u + 1)

        op_a(last)
        fill("g02", last)
        op_d(last)
        fill("g4", last)
        back(1, last - 1)
        x_copy(1, last - 1)
        for job in early[last]:
            job_pe(job)
            job_copy(job)
        op_h(last)
        back(1, last, kind="s")
        x_copy(1, last)
        back(0, last - 1)
        x_copy(0, last - 1)
        op_b(last)
        quant("yy", 2, (0, 1))
        y_fill(3, 1, 0)
        y_fill(3, 1, 1, kind="s")
        op_e(last)
        quant("xx", 3, (1,))
        y_copy(3, 1, 0)
        y_copy(3, 1, 1)
        for job in late[last]:
            job_pe(job)
            job_copy(job)
        op_c(last)
        op_m(last)
        op_f(last, nc.vector)
        for m in range(4):
            dw_passes(1, 1, m, kind=("s" if m == 1 else "back"))
            store(T["ow", 1, 1, m], out_2, 1, m)
            dx_passes(1, m, DX_ORDER[:2], kind="fwd")
        quant("yy", 3, (1,))
        op_g(last, nc.vector)
        back(0, last)
        x_copy(0, last)
        for m in range(2):
            dx_passes(1, m, DX_ORDER[2:3])
        y_fill(3, 0, 0)
        y_fill(3, 0, 1, kind="s")
        quant("xx", 3, (0,))
        y_copy(3, 0, 0)
        y_copy(3, 0, 1, eng="v")
        for m in range(2):
            dw_passes(0, 1, m)
        for m in range(2, 4):
            dx_passes(1, m, DX_ORDER[2:3])
        quant("yy", 3, (0,))
        for m in range(2):
            store(T["ow", 0, 1, m], out_1, 1, m)
        for m in range(2, 4):
            dw_passes(0, 1, m, kind=("s" if m == 3 else "back"))
        for m in range(4):
            dx_passes(1, m, DX_ORDER[3:])
        order = [("ow", 2, "v"), ("ow", 3, "v"), ("o0", 0, "s"), ("o0", 1, "v"), ("o0", 2, "s"), ("o0", 3, "v")]
        for kind, m, eng in order:
            if kind == "ow":
                store(T["ow", 0, 1, m], out_1, 1, m, eng=eng)
            else:
                store(T["o0", 1, m], out_0, 1, m, eng=eng)
